import numpy as np
import ml_dtypes


def mxq(x, axis, fmt="e4m3"):
    dtype, down = {"e4m3": (ml_dtypes.float8_e4m3fn, 7), "e5m2": (ml_dtypes.float8_e5m2, 14)}[fmt]
    v = np.moveaxis(np.asarray(x, np.float32).astype(ml_dtypes.bfloat16).astype(np.float64), axis, -1)
    blocks = v.reshape(v.shape[:-1] + (-1, 32))
    amax = np.abs(blocks).max(-1, keepdims=True)
    byte = np.maximum(np.where(amax > 0, np.frexp(amax)[1] - 1 + 127, 0) - down, 1)
    scale = np.exp2(byte - 127.0)
    codes = (blocks / scale).astype(np.float32).astype(dtype).astype(np.float64)
    return np.moveaxis((codes * scale).reshape(v.shape), -1, axis)


WIDE = False


def mx_kscale(k):
    if not WIDE:
        return np.ones(k)
    levels = np.array([10, -10, 5, -5, 0])
    if k % 512:
        return np.exp2(np.random.permutation(np.resize(levels, k // 32))).repeat(32)
    a = np.empty((k // 512, 16))
    for p in range(k // 512):
        a[p, :8] = np.random.permutation(np.resize(levels, 8))
        for g in range(8):
            far = levels[np.abs(levels - a[p, g]) >= 10]
            a[p, g + 8] = far[np.random.randint(len(far))]
    return np.exp2(a.ravel()).repeat(32)


BF16 = ml_dtypes.bfloat16


def bf(x):
    return np.asarray(x, np.float32).astype(BF16)


def f64(x):
    return np.asarray(x).astype(np.float64)


B, N, F = 1, 1024, 1024


def setup_inputs():
    s = mx_kscale(F)
    limit = np.sqrt(6.0 / (F + F))
    return {"nodes": bf(np.random.standard_normal((B, N, F)) * s),
            "W": bf(np.random.uniform(-limit, limit, (F, F)) / s[:, None] / s[None, :])}


def reference(nodes, W):
    norm_const = 1.0 / np.sqrt(F)
    nq = mxq(f64(nodes), 2, "e4m3")
    x = nq @ mxq(f64(W), 0, "e4m3")
    prods = mxq(x, 2, "e4m3") @ nq.transpose(0, 2, 1)
    z = prods * norm_const
    e = np.exp(z - z.max(-1, keepdims=True))
    return e / e.sum(-1, keepdims=True)

@@ -1,0 +1,208 @@
+from contextlib import ExitStack
+
+import concourse.mybir as mybir
+from concourse.masks import make_identity
+
+BF16 = mybir.dt.bfloat16
+F32 = mybir.dt.float32
+U32 = mybir.dt.uint32
+U8 = mybir.dt.uint8
+FP8X4 = mybir.dt.float8_e4m3fn_x4
+ACT = mybir.ActivationFunctionType
+ALU = mybir.AluOpType
+AXIS = mybir.AxisListType
+
+P = 128
+PACK = 4
+K_PASS = P * PACK
+NODES = 1024
+FEATURES = 1024
+PASSES = FEATURES // K_PASS
+BLOCKS = NODES // P
+BANK = 512
+HALVES = NODES // BANK
+LOOKAHEAD = 2
+
+FLOPS = 2 * 2 * NODES * FEATURES * FEATURES
+
+
+def tile_scalarproductattentiont_pa_kernel(tc, nodes, W, out):
+    nc = tc.nc
+    node_rows = nodes.flatten_outer_dims()
+    out_rows = out.flatten_outer_dims()
+
+    with ExitStack() as ctx:
+        keep = ctx.enter_context(tc.tile_pool(name="keep", bufs=1))
+        xpool = ctx.enter_context(tc.tile_pool(name="xpool", bufs=LOOKAHEAD + 2))
+        soft = ctx.enter_context(tc.tile_pool(name="soft", bufs=3))
+        banks = ctx.enter_context(tc.psum_pool(name="banks", bufs=8))
+
+        w_raw = keep.tile([P, PASSES, PACK, FEATURES], BF16)
+        for c in range(PASSES):
+            pass_rows = W[K_PASS * c : K_PASS * (c + 1), :]
+            nc.sync.dma_start(
+                out=w_raw[:, c, :, :],
+                in_=pass_rows.rearrange("(p t) g -> p t g", t=PACK),
+            )
+        n_raw = keep.tile([P, BLOCKS * FEATURES], BF16)
+        for b in range(BLOCKS):
+            nc.sync.dma_start(
+                out=n_raw[:, FEATURES * b : FEATURES * (b + 1)],
+                in_=node_rows[P * b : P * (b + 1), :],
+            )
+
+        ident = keep.tile([P, P], F32)
+        make_identity(nc, ident[:])
+
+        warm_in = keep.tile([P, 1], F32)
+        warm_out = keep.tile([P, 1], F32)
+        nc.vector.memset(warm_in[:], 0.0)
+        nc.scalar.activation(out=warm_out[:], in_=warm_in[:], func=ACT.Exp)
+
+        w_grouped = keep.tile([P, PASSES, PACK, 256 * PACK], BF16, align_bytes=64)
+        w_codes = keep.tile([P, PASSES, PACK, 256], U32, align_bytes=64)
+        w_scales = keep.tile([P, PASSES, PACK, 256], U8, align_bytes=64)
+        for c in range(PASSES):
+            for to in range(PACK):
+                dst = w_grouped[:, c, to, :].rearrange("p (r i t) -> p r t i", i=4, t=PACK)
+                src = w_raw[:, c, :, :].rearrange("p t (r i e) -> p e r t i", i=4, e=PACK)[:, to]
+                if to < 3:
+                    nc.vector.tensor_copy(out=dst, in_=src)
+                else:
+                    nc.scalar.copy(out=dst, in_=src)
+            for half in range(2):
+                pair = slice(2 * half, 2 * half + 2)
+                nc.vector.quantize_mx(
+                    out=w_codes[:, c, pair, :].rearrange("p e q -> p (e q)").bitcast(FP8X4),
+                    scales=w_scales[:, c, pair, :].rearrange("p e q -> p (e q)"),
+                    in_=w_grouped[:, c, pair, :].rearrange("p e q -> p (e q)"),
+                )
+
+        n_words = n_raw[:].bitcast(F32)
+        n_grouped = keep.tile([P, PASSES * NODES * PACK], BF16, align_bytes=64)
+        n_grouped_words = n_grouped[:].bitcast(F32).rearrange(
+            "p (c n u) -> p c n u", c=PASSES, u=2
+        )
+        n_codes = keep.tile([P, PASSES, NODES], U32, align_bytes=64)
+        n_scales = keep.tile([P, PASSES, NODES], U8, align_bytes=64)
+        for b in range(BLOCKS):
+            flipped = banks.tile([P, PASSES, 2, P], F32, tag="bank")
+            for c in range(PASSES):
+                for u in range(2):
+                    first_word = 512 * b + 256 * c
+                    nc.tensor.transpose(
+                        flipped[:, c, u, :],
+                        n_words[:, first_word + u : first_word + 2 * P : 2],
+                        ident[:],
+                    )
+            nc.scalar.copy(
+                out=n_grouped_words[:, :, P * b : P * (b + 1), :],
+                in_=flipped[:].rearrange("p c u n -> p c n u"),
+            )
+            if b % 2 == 1:
+                first_node = P * (b - 1)
+                for c in range(PASSES):
+                    start = PACK * (NODES * c + first_node)
+                    nc.vector.quantize_mx(
+                        out=n_codes[:, c, first_node : first_node + 2 * P].bitcast(FP8X4),
+                        scales=n_scales[:, c, first_node : first_node + 2 * P],
+                        in_=n_grouped[:, start : start + 2 * P * PACK],
+                    )
+
+        def first_matmul(b):
+            x_grouped = xpool.tile([P, PASSES, P, PACK], BF16, align_bytes=64)
+            for co in range(PASSES):
+                xt = banks.tile([P, PACK, P], F32, tag="bank")
+                for t in range(PACK):
+                    first = P * co
+                    for c in range(PASSES):
+                        nc.tensor.matmul_mx(
+                            out=xt[:, t, :],
+                            lhsT=w_codes[:, c, t, first : first + P].bitcast(FP8X4),
+                            lhsT_scale=w_scales[:, c, t, first : first + P],
+                            rhs=n_codes[:, c, P * b : P * (b + 1)].bitcast(FP8X4),
+                            rhs_scale=n_scales[:, c, P * b : P * (b + 1)],
+                            start=(c == 0),
+                            stop=(c == PASSES - 1),
+                        )
+                if co == 0:
+                    nc.vector.tensor_copy(
+                        out=x_grouped[:, co, :, :], in_=xt[:].rearrange("p t n -> p n t")
+                    )
+                else:
+                    nc.scalar.copy(
+                        out=x_grouped[:, co, :, :], in_=xt[:].rearrange("p t n -> p n t")
+                    )
+            x_codes = xpool.tile([P, PASSES, P], U32, align_bytes=64)
+            x_scales = xpool.tile([P, PASSES, P], U8, align_bytes=64)
+            nc.vector.quantize_mx(
+                out=x_codes[:].rearrange("p c n -> p (c n)").bitcast(FP8X4),
+                scales=x_scales[:].rearrange("p c n -> p (c n)"),
+                in_=x_grouped[:].rearrange("p c n t -> p (c n t)"),
+            )
+            return x_codes, x_scales
+
+        def second_matmul_and_softmax(b, x_codes, x_scales):
+            prods = []
+            row_max = soft.tile([P, HALVES], F32)
+            for h in range(HALVES):
+                prod = banks.tile([P, BANK], F32, tag="bank")
+                for c in range(PASSES):
+                    nc.tensor.matmul_mx(
+                        out=prod[:],
+                        lhsT=x_codes[:, c, :].bitcast(FP8X4),
+                        lhsT_scale=x_scales[:, c, :],
+                        rhs=n_codes[:, c, BANK * h : BANK * (h + 1)].bitcast(FP8X4),
+                        rhs_scale=n_scales[:, c, BANK * h : BANK * (h + 1)],
+                        start=(c == 0),
+                        stop=(c == PASSES - 1),
+                    )
+                nc.vector.tensor_reduce(
+                    out=row_max[:, h : h + 1], in_=prod[:], axis=AXIS.X, op=ALU.max
+                )
+                prods.append(prod)
+            shift = soft.tile([P, 1], F32)
+            nc.vector.tensor_scalar(
+                out=shift[:],
+                in0=row_max[:, 0:1],
+                scalar1=row_max[:, 1:2],
+                scalar2=-1.0 / 32.0,
+                op0=ALU.max,
+                op1=ALU.mult,
+            )
+            expd = soft.tile([P, NODES], F32)
+            part_sum = soft.tile([P, HALVES], F32)
+            for h in range(HALVES):
+                nc.scalar.activation(
+                    out=expd[:, BANK * h : BANK * (h + 1)],
+                    in_=prods[h][:],
+                    func=ACT.Exp,
+                    bias=shift[:, 0:1],
+                    scale=1.0 / 32.0,
+                    accum_out=part_sum[:, h : h + 1],
+                )
+            row_sum = soft.tile([P, 1], F32)
+            nc.vector.tensor_reduce(out=row_sum[:], in_=part_sum[:], axis=AXIS.X, op=ALU.add)
+            inv_sum = soft.tile([P, 1], F32)
+            nc.vector.reciprocal(out=inv_sum[:], in_=row_sum[:])
+            weights = soft.tile([P, NODES], F32)
+            for h in range(HALVES):
+                cols = slice(BANK * h, BANK * (h + 1))
+                nc.gpsimd.tensor_scalar(
+                    out=weights[:, cols],
+                    in0=expd[:, cols],
+                    scalar1=inv_sum[:, 0:1],
+                    scalar2=0.0,
+                    op0=ALU.mult,
+                    op1=ALU.add,
+                )
+                nc.sync.dma_start(out=out_rows[P * b : P * (b + 1), cols], in_=weights[:, cols])
+
+        x_ready = []
+        for b in range(LOOKAHEAD):
+            x_ready.append(first_matmul(b))
+        for b in range(BLOCKS):
+            if b + LOOKAHEAD < BLOCKS:
+                x_ready.append(first_matmul(b + LOOKAHEAD))
+            x_codes, x_scales = x_ready[b]
+            second_matmul_and_softmax(b, x_codes, x_scales)

@@ -18,10 +18,10 @@ K_PASS = P * PACK
 NODES = 1024
 FEATURES = 1024
 PASSES = FEATURES // K_PASS
+GROUPS = FEATURES // K_PASS
 BLOCKS = NODES // P
 BANK = 512
 HALVES = NODES // BANK
-LOOKAHEAD = 2
 
 FLOPS = 2 * 2 * NODES * FEATURES * FEATURES
 
@@ -33,176 +33,253 @@ def tile_scalarproductattentiont_pa_kernel(tc, nodes, W, out):
 
     with ExitStack() as ctx:
         keep = ctx.enter_context(tc.tile_pool(name="keep", bufs=1))
-        xpool = ctx.enter_context(tc.tile_pool(name="xpool", bufs=LOOKAHEAD + 2))
         soft = ctx.enter_context(tc.tile_pool(name="soft", bufs=3))
-        banks = ctx.enter_context(tc.psum_pool(name="banks", bufs=8))
+        x_banks = ctx.enter_context(tc.psum_pool(name="x_banks", bufs=3))
+        banks = ctx.enter_context(tc.psum_pool(name="banks", bufs=5))
+        ctx.enter_context(tc.manual_schedule())
 
-        w_raw = keep.tile([P, PASSES, PACK, FEATURES], BF16)
-        for c in range(PASSES):
-            pass_rows = W[K_PASS * c : K_PASS * (c + 1), :]
-            nc.sync.dma_start(
-                out=w_raw[:, c, :, :],
-                in_=pass_rows.rearrange("(p t) g -> p t g", t=PACK),
-            )
-        n_raw = keep.tile([P, BLOCKS * FEATURES], BF16)
+        w_raw = keep.tile([P, PASSES, GROUPS, PACK, BANK], BF16, name="w_raw")
+        w_grouped = keep.tile([P, PASSES, GROUPS, PACK, P * PACK], BF16, align_bytes=64, name="w_grouped")
+        w_codes = keep.tile([P, PASSES, GROUPS, PACK, P], U32, align_bytes=64, name="w_codes")
+        w_scales = keep.tile([P, PASSES, GROUPS, PACK, P], U8, align_bytes=64, name="w_scales")
+        n_raw = keep.tile([P, BLOCKS, FEATURES], BF16, name="n_raw")
+        n_words = n_raw[:].rearrange("p b f -> p (b f)").bitcast(F32)
+        n_grouped = keep.tile([P, PASSES * NODES * PACK], BF16, align_bytes=64, name="n_grouped")
+        n_grouped_words = n_grouped[:].bitcast(F32).rearrange("p (c n u) -> p c n u", c=PASSES, u=2)
+        n_codes = keep.tile([P, PASSES, NODES], U32, align_bytes=64, name="n_codes")
+        n_scales = keep.tile([P, PASSES, NODES], U8, align_bytes=64, name="n_scales")
+        x_grouped = keep.tile([P, BLOCKS, GROUPS, P, PACK], BF16, align_bytes=64, name="x_grouped")
+        x_codes = keep.tile([P, BLOCKS, GROUPS, P], U32, align_bytes=64, name="x_codes")
+        x_scales = keep.tile([P, BLOCKS, GROUPS, P], U8, align_bytes=64, name="x_scales")
+
+        def load_w(co):
+            for c in range(PASSES):
+                nc.sync.dma_start(
+                    out=w_raw[:, c, co, :, :],
+                    in_=W[K_PASS * c : K_PASS * (c + 1), BANK * co : BANK * (co + 1)].rearrange(
+                        "(p t) g -> p t g", t=PACK
+                    ),
+                )
+
+        load_w(0)
         for b in range(BLOCKS):
-            nc.sync.dma_start(
-                out=n_raw[:, FEATURES * b : FEATURES * (b + 1)],
-                in_=node_rows[P * b : P * (b + 1), :],
-            )
+            nc.sync.dma_start(out=n_raw[:, b, :], in_=node_rows[P * b : P * (b + 1), :])
+        load_w(1)
 
-        ident = keep.tile([P, P], F32)
+        ident = keep.tile([P, P], F32, name="ident")
         make_identity(nc, ident[:])
 
-        warm_in = keep.tile([P, 1], F32)
-        warm_out = keep.tile([P, 1], F32)
+        warm_in = keep.tile([P, 1], F32, name="warm_in")
+        warm_out = keep.tile([P, 1], F32, name="warm_out")
         nc.vector.memset(warm_in[:], 0.0)
         nc.scalar.activation(out=warm_out[:], in_=warm_in[:], func=ACT.Exp)
 
-        w_grouped = keep.tile([P, PASSES, PACK, 256 * PACK], BF16, align_bytes=64)
-        w_codes = keep.tile([P, PASSES, PACK, 256], U32, align_bytes=64)
-        w_scales = keep.tile([P, PASSES, PACK, 256], U8, align_bytes=64)
-        for c in range(PASSES):
-            for to in range(PACK):
-                dst = w_grouped[:, c, to, :].rearrange("p (r i t) -> p r t i", i=4, t=PACK)
-                src = w_raw[:, c, :, :].rearrange("p t (r i e) -> p e r t i", i=4, e=PACK)[:, to]
-                if to < 3:
-                    nc.vector.tensor_copy(out=dst, in_=src)
-                else:
-                    nc.scalar.copy(out=dst, in_=src)
-            for half in range(2):
-                pair = slice(2 * half, 2 * half + 2)
-                nc.vector.quantize_mx(
-                    out=w_codes[:, c, pair, :].rearrange("p e q -> p (e q)").bitcast(FP8X4),
-                    scales=w_scales[:, c, pair, :].rearrange("p e q -> p (e q)"),
-                    in_=w_grouped[:, c, pair, :].rearrange("p e q -> p (e q)"),
-                )
+        def regroup_w(engine_copy, c, co, t):
+            engine_copy(
+                out=w_grouped[:, c, co, t, :].rearrange("p (r i j) -> p r j i", i=4, j=PACK),
+                in_=w_raw[:, c, co, :, :].rearrange("p j (r i t) -> p t r j i", i=4, t=PACK)[:, t],
+            )
 
-        n_words = n_raw[:].bitcast(F32)
-        n_grouped = keep.tile([P, PASSES * NODES * PACK], BF16, align_bytes=64)
-        n_grouped_words = n_grouped[:].bitcast(F32).rearrange(
-            "p (c n u) -> p c n u", c=PASSES, u=2
-        )
-        n_codes = keep.tile([P, PASSES, NODES], U32, align_bytes=64)
-        n_scales = keep.tile([P, PASSES, NODES], U8, align_bytes=64)
-        for b in range(BLOCKS):
-            flipped = banks.tile([P, PASSES, 2, P], F32, tag="bank")
+        def quantise_w(c, co, pair):
+            ts = slice(2 * pair, 2 * pair + 2)
+            nc.vector.quantize_mx(
+                out=w_codes[:, c, co, ts, :].rearrange("p t q -> p (t q)").bitcast(FP8X4),
+                scales=w_scales[:, c, co, ts, :].rearrange("p t q -> p (t q)"),
+                in_=w_grouped[:, c, co, ts, :].rearrange("p t q -> p (t q)"),
+            )
+
+        def prepare_w(c, co):
+            for t in (2, 3):
+                regroup_w(nc.scalar.copy, c, co, t)
+            for t in (0, 1):
+                regroup_w(nc.vector.tensor_copy, c, co, t)
+            for pair in range(2):
+                quantise_w(c, co, pair)
+
+        flipped = {}
+
+        def transpose_nodes(b):
+            flipped[b] = banks.tile([P, PASSES, 2, P], F32, tag="bank", name="flip")
             for c in range(PASSES):
                 for u in range(2):
                     first_word = 512 * b + 256 * c
                     nc.tensor.transpose(
-                        flipped[:, c, u, :],
+                        flipped[b][:, c, u, :],
                         n_words[:, first_word + u : first_word + 2 * P : 2],
                         ident[:],
                     )
-            nc.scalar.copy(
+
+        def copy_nodes(engine_copy, b):
+            engine_copy(
                 out=n_grouped_words[:, :, P * b : P * (b + 1), :],
-                in_=flipped[:].rearrange("p c u n -> p c n u"),
+                in_=flipped[b][:].rearrange("p c u n -> p c n u"),
             )
-            if b % 2 == 1:
-                first_node = P * (b - 1)
-                for c in range(PASSES):
-                    start = PACK * (NODES * c + first_node)
-                    nc.vector.quantize_mx(
-                        out=n_codes[:, c, first_node : first_node + 2 * P].bitcast(FP8X4),
-                        scales=n_scales[:, c, first_node : first_node + 2 * P],
-                        in_=n_grouped[:, start : start + 2 * P * PACK],
-                    )
 
-        def first_matmul(b):
-            x_grouped = xpool.tile([P, PASSES, P, PACK], BF16, align_bytes=64)
-            for co in range(PASSES):
-                xt = banks.tile([P, PACK, P], F32, tag="bank")
-                for t in range(PACK):
-                    first = P * co
-                    for c in range(PASSES):
-                        nc.tensor.matmul_mx(
-                            out=xt[:, t, :],
-                            lhsT=w_codes[:, c, t, first : first + P].bitcast(FP8X4),
-                            lhsT_scale=w_scales[:, c, t, first : first + P],
-                            rhs=n_codes[:, c, P * b : P * (b + 1)].bitcast(FP8X4),
-                            rhs_scale=n_scales[:, c, P * b : P * (b + 1)],
-                            start=(c == 0),
-                            stop=(c == PASSES - 1),
-                        )
-                if co == 0:
-                    nc.vector.tensor_copy(
-                        out=x_grouped[:, co, :, :], in_=xt[:].rearrange("p t n -> p n t")
-                    )
-                else:
-                    nc.scalar.copy(
-                        out=x_grouped[:, co, :, :], in_=xt[:].rearrange("p t n -> p n t")
-                    )
-            x_codes = xpool.tile([P, PASSES, P], U32, align_bytes=64)
-            x_scales = xpool.tile([P, PASSES, P], U8, align_bytes=64)
-            nc.vector.quantize_mx(
-                out=x_codes[:].rearrange("p c n -> p (c n)").bitcast(FP8X4),
-                scales=x_scales[:].rearrange("p c n -> p (c n)"),
-                in_=x_grouped[:].rearrange("p c n t -> p (c n t)"),
-            )
-            return x_codes, x_scales
+        def quantise_nodes(b):
+            for c in range(PASSES):
+                start = PACK * (NODES * c + P * b)
+                nc.vector.quantize_mx(
+                    out=n_codes[:, c, P * b : P * (b + 1)].bitcast(FP8X4),
+                    scales=n_scales[:, c, P * b : P * (b + 1)],
+                    in_=n_grouped[:, start : start + P * PACK],
+                )
 
-        def second_matmul_and_softmax(b, x_codes, x_scales):
-            prods = []
-            row_max = soft.tile([P, HALVES], F32)
-            for h in range(HALVES):
-                prod = banks.tile([P, BANK], F32, tag="bank")
+        xt = {}
+
+        def first_matmul(b, co):
+            xt[b, co] = x_banks.tile([P, PACK, P], F32, tag="xt", name="xt")
+            for t in range(PACK):
                 for c in range(PASSES):
                     nc.tensor.matmul_mx(
-                        out=prod[:],
-                        lhsT=x_codes[:, c, :].bitcast(FP8X4),
-                        lhsT_scale=x_scales[:, c, :],
-                        rhs=n_codes[:, c, BANK * h : BANK * (h + 1)].bitcast(FP8X4),
-                        rhs_scale=n_scales[:, c, BANK * h : BANK * (h + 1)],
+                        out=xt[b, co][:, t, :],
+                        lhsT=w_codes[:, c, co, t, :].bitcast(FP8X4),
+                        lhsT_scale=w_scales[:, c, co, t, :],
+                        rhs=n_codes[:, c, P * b : P * (b + 1)].bitcast(FP8X4),
+                        rhs_scale=n_scales[:, c, P * b : P * (b + 1)],
                         start=(c == 0),
                         stop=(c == PASSES - 1),
                     )
-                nc.vector.tensor_reduce(
-                    out=row_max[:, h : h + 1], in_=prod[:], axis=AXIS.X, op=ALU.max
+
+        def copy_x(engine_copy, b, co):
+            engine_copy(
+                out=x_grouped[:, b, co, :, :], in_=xt[b, co][:].rearrange("p t n -> p n t")
+            )
+
+        def quantise_x(b, co):
+            nc.vector.quantize_mx(
+                out=x_codes[:, b, co, :].bitcast(FP8X4),
+                scales=x_scales[:, b, co, :],
+                in_=x_grouped[:, b, co, :, :].rearrange("p n t -> p (n t)"),
+            )
+
+        prods = {}
+        row_max = {}
+        shift = {}
+
+        def second_matmul(b, h):
+            prods[b, h] = banks.tile([P, BANK], F32, tag="bank", name="prod")
+            for c in range(PASSES):
+                nc.tensor.matmul_mx(
+                    out=prods[b, h][:],
+                    lhsT=x_codes[:, b, c, :].bitcast(FP8X4),
+                    lhsT_scale=x_scales[:, b, c, :],
+                    rhs=n_codes[:, c, BANK * h : BANK * (h + 1)].bitcast(FP8X4),
+                    rhs_scale=n_scales[:, c, BANK * h : BANK * (h + 1)],
+                    start=(c == 0),
+                    stop=(c == PASSES - 1),
                 )
-                prods.append(prod)
-            shift = soft.tile([P, 1], F32)
+
+        def half_max(b, h):
+            if h == 0:
+                row_max[b] = soft.tile([P, HALVES], F32, name="row_max")
+            nc.vector.tensor_reduce(
+                out=row_max[b][:, h : h + 1], in_=prods[b, h][:], axis=AXIS.X, op=ALU.max
+            )
+
+        def find_shift(b):
+            shift[b] = soft.tile([P, 1], F32, name="shift")
             nc.vector.tensor_scalar(
-                out=shift[:],
-                in0=row_max[:, 0:1],
-                scalar1=row_max[:, 1:2],
+                out=shift[b][:],
+                in0=row_max[b][:, 0:1],
+                scalar1=row_max[b][:, 1:2],
                 scalar2=-1.0 / 32.0,
                 op0=ALU.max,
                 op1=ALU.mult,
             )
-            expd = soft.tile([P, NODES], F32)
-            part_sum = soft.tile([P, HALVES], F32)
-            for h in range(HALVES):
-                nc.scalar.activation(
-                    out=expd[:, BANK * h : BANK * (h + 1)],
-                    in_=prods[h][:],
-                    func=ACT.Exp,
-                    bias=shift[:, 0:1],
-                    scale=1.0 / 32.0,
-                    accum_out=part_sum[:, h : h + 1],
-                )
-            row_sum = soft.tile([P, 1], F32)
-            nc.vector.tensor_reduce(out=row_sum[:], in_=part_sum[:], axis=AXIS.X, op=ALU.add)
-            inv_sum = soft.tile([P, 1], F32)
-            nc.vector.reciprocal(out=inv_sum[:], in_=row_sum[:])
-            weights = soft.tile([P, NODES], F32)
+
+        expd = {}
+        part_sum = {}
+        inv_sum = {}
+
+        def exponential(b, h):
+            if h == 0:
+                expd[b] = soft.tile([P, NODES], F32, name="expd")
+                part_sum[b] = soft.tile([P, HALVES], F32, name="part_sum")
+            nc.scalar.activation(
+                out=expd[b][:, BANK * h : BANK * (h + 1)],
+                in_=prods[b, h][:],
+                func=ACT.Exp,
+                bias=shift[b][:, 0:1],
+                scale=1.0 / 32.0,
+                accum_out=part_sum[b][:, h : h + 1],
+            )
+
+        row_sum = {}
+
+        def add_sums(b):
+            row_sum[b] = soft.tile([P, 1], F32, name="row_sum")
+            nc.vector.tensor_reduce(out=row_sum[b][:], in_=part_sum[b][:], axis=AXIS.X, op=ALU.add)
+
+        def invert_sum(b):
+            inv_sum[b] = soft.tile([P, 1], F32, name="inv_sum")
+            nc.vector.reciprocal(out=inv_sum[b][:], in_=row_sum[b][:])
+
+        def normalise(engine, b):
+            weights = soft.tile([P, NODES], F32, name="weights")
             for h in range(HALVES):
                 cols = slice(BANK * h, BANK * (h + 1))
-                nc.gpsimd.tensor_scalar(
+                engine.tensor_scalar(
                     out=weights[:, cols],
-                    in0=expd[:, cols],
-                    scalar1=inv_sum[:, 0:1],
+                    in0=expd[b][:, cols],
+                    scalar1=inv_sum[b][:, 0:1],
                     scalar2=0.0,
                     op0=ALU.mult,
                     op1=ALU.add,
                 )
                 nc.sync.dma_start(out=out_rows[P * b : P * (b + 1), cols], in_=weights[:, cols])
 
-        x_ready = []
-        for b in range(LOOKAHEAD):
-            x_ready.append(first_matmul(b))
-        for b in range(BLOCKS):
-            if b + LOOKAHEAD < BLOCKS:
-                x_ready.append(first_matmul(b + LOOKAHEAD))
-            x_codes, x_scales = x_ready[b]
-            second_matmul_and_softmax(b, x_codes, x_scales)
+        for c in range(PASSES):
+            prepare_w(c, 0)
+        pairs = BLOCKS // 2
+        for k in range(pairs + 1):
+            if k < pairs:
+                for b in (2 * k, 2 * k + 1):
+                    transpose_nodes(b)
+                    copy_nodes(nc.scalar.copy, b)
+            if k > 0:
+                first_matmul(2 * k - 2, 0)
+                first_matmul(2 * k - 1, 0)
+            if k < pairs:
+                quantise_nodes(2 * k)
+                quantise_nodes(2 * k + 1)
+            if k > 0:
+                copy_x(nc.vector.tensor_copy, 2 * k - 2, 0)
+                copy_x(nc.scalar.copy, 2 * k - 1, 0)
+            if k >= 2 and k < 2 + PASSES:
+                prepare_w(k - 2, 1)
+            if k > 1:
+                quantise_x(2 * k - 4, 0)
+                quantise_x(2 * k - 3, 0)
+        for b in (BLOCKS - 2, BLOCKS - 1):
+            quantise_x(b, 0)
+
+        for step in range(BLOCKS + 3):
+            if step < BLOCKS:
+                first_matmul(step, 1)
+                copy_x(nc.vector.tensor_copy if step % 4 == 3 else nc.scalar.copy, step, 1)
+            b = step - 1
+            if 0 <= b < BLOCKS:
+                second_matmul(b, 0)
+                half_max(b, 0)
+            if step < BLOCKS:
+                quantise_x(step, 1)
+            if 0 <= b < BLOCKS:
+                second_matmul(b, 1)
+                half_max(b, 1)
+            b = step - 3
+            if 0 <= b < BLOCKS:
+                add_sums(b)
+            b = step - 1
+            if 0 <= b < BLOCKS:
+                find_shift(b)
+            b = step - 3
+            if 0 <= b < BLOCKS:
+                invert_sum(b)
+                if b < BLOCKS - 1:
+                    normalise(nc.gpsimd, b)
+                else:
+                    normalise(nc.vector, b)
+            b = step - 2
+            if 0 <= b < BLOCKS:
+                for h in range(HALVES):
+                    exponential(b, h)

@@ -52,19 +52,27 @@ def tile_scalarproductattentiont_pa_kernel(tc, nodes, W, out):
         x_codes = keep.tile([P, BLOCKS, GROUPS, P], U32, align_bytes=64, name="x_codes")
         x_scales = keep.tile([P, BLOCKS, GROUPS, P], U8, align_bytes=64, name="x_scales")
 
-        def load_w(co):
-            for c in range(PASSES):
-                nc.sync.dma_start(
-                    out=w_raw[:, c, co, :, :],
-                    in_=W[K_PASS * c : K_PASS * (c + 1), BANK * co : BANK * (co + 1)].rearrange(
-                        "(p t) g -> p t g", t=PACK
-                    ),
-                )
+        def load_w(c, co):
+            nc.sync.dma_start(
+                out=w_raw[:, c, co, :, :],
+                in_=W[K_PASS * c : K_PASS * (c + 1), BANK * co : BANK * (co + 1)].rearrange(
+                    "(p t) g -> p t g", t=PACK
+                ),
+            )
 
-        load_w(0)
-        for b in range(BLOCKS):
+        def load_nodes(b):
             nc.sync.dma_start(out=n_raw[:, b, :], in_=node_rows[P * b : P * (b + 1), :])
-        load_w(1)
+
+        load_nodes(0)
+        load_nodes(1)
+        load_w(0, 0)
+        load_w(1, 0)
+        load_nodes(2)
+        load_nodes(3)
+        load_w(0, 1)
+        for b in range(4, 8):
+            load_nodes(b)
+        load_w(1, 1)
 
         ident = keep.tile([P, P], F32, name="ident")
         make_identity(nc, ident[:])
@@ -89,10 +97,15 @@ def tile_scalarproductattentiont_pa_kernel(tc, nodes, W, out):
             )
 
         def prepare_w(c, co):
-            for t in (2, 3):
-                regroup_w(nc.scalar.copy, c, co, t)
-            for t in (0, 1):
-                regroup_w(nc.vector.tensor_copy, c, co, t)
+            regroup(c, co)
+            quantise(c, co)
+
+        def regroup(c, co):
+            for t in range(PACK):
+                shared = co == 0 and t >= 2
+                regroup_w(nc.scalar.copy if shared else nc.vector.tensor_copy, c, co, t)
+
+        def quantise(c, co):
             for pair in range(2):
                 quantise_w(c, co, pair)
 
@@ -115,13 +128,13 @@ def tile_scalarproductattentiont_pa_kernel(tc, nodes, W, out):
                 in_=flipped[b][:].rearrange("p c u n -> p c n u"),
             )
 
-        def quantise_nodes(b):
+        def quantise_nodes(b, count):
             for c in range(PASSES):
                 start = PACK * (NODES * c + P * b)
                 nc.vector.quantize_mx(
-                    out=n_codes[:, c, P * b : P * (b + 1)].bitcast(FP8X4),
-                    scales=n_scales[:, c, P * b : P * (b + 1)],
-                    in_=n_grouped[:, start : start + P * PACK],
+                    out=n_codes[:, c, P * b : P * (b + count)].bitcast(FP8X4),
+                    scales=n_scales[:, c, P * b : P * (b + count)],
+                    in_=n_grouped[:, start : start + count * P * PACK],
                 )
 
         xt = {}
@@ -153,7 +166,6 @@ def tile_scalarproductattentiont_pa_kernel(tc, nodes, W, out):
             )
 
         prods = {}
-        row_max = {}
         shift = {}
 
         def second_matmul(b, h):
@@ -169,23 +181,19 @@ def tile_scalarproductattentiont_pa_kernel(tc, nodes, W, out):
                     stop=(c == PASSES - 1),
                 )
 
-        def half_max(b, h):
-            if h == 0:
-                row_max[b] = soft.tile([P, HALVES], F32, name="row_max")
-            nc.vector.tensor_reduce(
-                out=row_max[b][:, h : h + 1], in_=prods[b, h][:], axis=AXIS.X, op=ALU.max
-            )
-
-        def find_shift(b):
-            shift[b] = soft.tile([P, 1], F32, name="shift")
+        def find_shift(b, h):
+            new = soft.tile([P, 1], F32, name="shift%d" % h)
+            scaled = soft.tile([P, BANK], F32, name="scaled")
             nc.vector.tensor_scalar(
-                out=shift[b][:],
-                in0=row_max[b][:, 0:1],
-                scalar1=row_max[b][:, 1:2],
-                scalar2=-1.0 / 32.0,
-                op0=ALU.max,
-                op1=ALU.mult,
+                out=scaled[:],
+                in0=prods[b, h][:],
+                scalar1=-1.0 / 32.0,
+                scalar2=None if h == 0 else shift[b][:, 0:1],
+                op0=ALU.mult,
+                op1=ALU.min,
+                accum_out=new[:],
             )
+            shift[b] = new
 
         expd = {}
         part_sum = {}
@@ -215,7 +223,7 @@ def tile_scalarproductattentiont_pa_kernel(tc, nodes, W, out):
             nc.vector.reciprocal(out=inv_sum[b][:], in_=row_sum[b][:])
 
         def normalise(engine, b):
-            weights = soft.tile([P, NODES], F32, name="weights")
+            weights = soft.tile([P, NODES], F32, name="weights", bufs=5)
             for h in range(HALVES):
                 cols = slice(BANK * h, BANK * (h + 1))
                 engine.tensor_scalar(
@@ -228,57 +236,60 @@ def tile_scalarproductattentiont_pa_kernel(tc, nodes, W, out):
                 )
                 nc.sync.dma_start(out=out_rows[P * b : P * (b + 1), cols], in_=weights[:, cols])
 
-        for c in range(PASSES):
-            prepare_w(c, 0)
         pairs = BLOCKS // 2
         for k in range(pairs + 1):
             if k < pairs:
                 for b in (2 * k, 2 * k + 1):
                     transpose_nodes(b)
                     copy_nodes(nc.scalar.copy, b)
+                if k == 0:
+                    quantise_nodes(0, 1)
+                    quantise_nodes(1, 1)
+                    for c in range(PASSES):
+                        prepare_w(c, 0)
+                else:
+                    if k == 3:
+                        regroup(1, 1)
+                    quantise_nodes(2 * k, 2)
+                    if k == 3:
+                        quantise(1, 1)
             if k > 0:
-                first_matmul(2 * k - 2, 0)
-                first_matmul(2 * k - 1, 0)
-            if k < pairs:
-                quantise_nodes(2 * k)
-                quantise_nodes(2 * k + 1)
-            if k > 0:
-                copy_x(nc.vector.tensor_copy, 2 * k - 2, 0)
-                copy_x(nc.scalar.copy, 2 * k - 1, 0)
-            if k >= 2 and k < 2 + PASSES:
-                prepare_w(k - 2, 1)
+                for b in (2 * k - 2, 2 * k - 1):
+                    if b == BLOCKS - 1:
+                        first_matmul(0, 1)
+                        copy_x(nc.scalar.copy, 0, 1)
+                    first_matmul(b, 0)
+                    copy_x(nc.scalar.copy, b, 0)
+            if k == 1:
+                prepare_w(0, 1)
             if k > 1:
                 quantise_x(2 * k - 4, 0)
                 quantise_x(2 * k - 3, 0)
-        for b in (BLOCKS - 2, BLOCKS - 1):
-            quantise_x(b, 0)
+        quantise_x(BLOCKS - 2, 0)
+        quantise_x(0, 1)
+        quantise_x(BLOCKS - 1, 0)
 
-        for step in range(BLOCKS + 3):
+        for step in range(1, BLOCKS + 3):
             if step < BLOCKS:
                 first_matmul(step, 1)
-                copy_x(nc.vector.tensor_copy if step % 4 == 3 else nc.scalar.copy, step, 1)
+                copy_x(nc.vector.tensor_copy if step % 4 == 1 else nc.scalar.copy, step, 1)
             b = step - 1
             if 0 <= b < BLOCKS:
                 second_matmul(b, 0)
-                half_max(b, 0)
+                find_shift(b, 0)
             if step < BLOCKS:
                 quantise_x(step, 1)
-            if 0 <= b < BLOCKS:
-                second_matmul(b, 1)
-                half_max(b, 1)
             b = step - 3
             if 0 <= b < BLOCKS:
                 add_sums(b)
             b = step - 1
             if 0 <= b < BLOCKS:
-                find_shift(b)
+                second_matmul(b, 1)
+                find_shift(b, 1)
             b = step - 3
             if 0 <= b < BLOCKS:
                 invert_sum(b)
-                if b < BLOCKS - 1:
-                    normalise(nc.gpsimd, b)
-                else:
-                    normalise(nc.vector, b)
+                normalise(nc.gpsimd if b < BLOCKS - 2 else nc.vector, b)
             b = step - 2
             if 0 <= b < BLOCKS:
                 for h in range(HALVES):

@@ -216,7 +216,12 @@ def tile_scalarproductattentiont_pa_kernel(tc, nodes, W, out):
 
         def add_sums(b):
             row_sum[b] = soft.tile([P, 1], F32, name="row_sum")
-            nc.vector.tensor_reduce(out=row_sum[b][:], in_=part_sum[b][:], axis=AXIS.X, op=ALU.add)
+            nc.scalar.activation(
+                out=row_sum[b][:],
+                in_=part_sum[b][:, 0:1],
+                func=ACT.Identity,
+                bias=part_sum[b][:, 1:2],
+            )
 
         def invert_sum(b):
             inv_sum[b] = soft.tile([P, 1], F32, name="inv_sum")
@@ -269,28 +274,26 @@ def tile_scalarproductattentiont_pa_kernel(tc, nodes, W, out):
         quantise_x(0, 1)
         quantise_x(BLOCKS - 1, 0)
 
-        for step in range(1, BLOCKS + 3):
+        for step in range(BLOCKS + 2):
+            i = step + 1
+            if i < BLOCKS:
+                first_matmul(i, 1)
+                copy_x(nc.vector.tensor_copy if i % 4 == 1 else nc.scalar.copy, i, 1)
             if step < BLOCKS:
-                first_matmul(step, 1)
-                copy_x(nc.vector.tensor_copy if step % 4 == 1 else nc.scalar.copy, step, 1)
-            b = step - 1
-            if 0 <= b < BLOCKS:
-                second_matmul(b, 0)
-                find_shift(b, 0)
-            if step < BLOCKS:
-                quantise_x(step, 1)
-            b = step - 3
-            if 0 <= b < BLOCKS:
-                add_sums(b)
-            b = step - 1
-            if 0 <= b < BLOCKS:
-                second_matmul(b, 1)
-                find_shift(b, 1)
-            b = step - 3
-            if 0 <= b < BLOCKS:
-                invert_sum(b)
-                normalise(nc.gpsimd if b < BLOCKS - 2 else nc.vector, b)
+                second_matmul(step, 0)
+                find_shift(step, 0)
+            if i < BLOCKS:
+                quantise_x(i, 1)
             b = step - 2
+            if b >= 0:
+                invert_sum(b)
+            if step < BLOCKS:
+                second_matmul(step, 1)
+                find_shift(step, 1)
+            if b >= 0:
+                normalise(nc.gpsimd if b < BLOCKS - 2 else nc.vector, b)
+            b = step - 1
             if 0 <= b < BLOCKS:
                 for h in range(HALVES):
                     exponential(b, h)
+                add_sums(b)

@@ -63,16 +63,18 @@ def tile_scalarproductattentiont_pa_kernel(tc, nodes, W, out):
         def load_nodes(b):
             nc.sync.dma_start(out=n_raw[:, b, :], in_=node_rows[P * b : P * (b + 1), :])
 
-        load_nodes(0)
-        load_nodes(1)
         load_w(0, 0)
         load_w(1, 0)
+        load_nodes(0)
+        load_nodes(1)
         load_nodes(2)
         load_nodes(3)
         load_w(0, 1)
-        for b in range(4, 8):
-            load_nodes(b)
+        load_nodes(4)
+        load_nodes(5)
         load_w(1, 1)
+        load_nodes(6)
+        load_nodes(7)
 
         ident = keep.tile([P, P], F32, name="ident")
         make_identity(nc, ident[:])
@@ -158,11 +160,11 @@ def tile_scalarproductattentiont_pa_kernel(tc, nodes, W, out):
                 out=x_grouped[:, b, co, :, :], in_=xt[b, co][:].rearrange("p t n -> p n t")
             )
 
-        def quantise_x(b, co):
+        def quantise_x(b, groups):
             nc.vector.quantize_mx(
-                out=x_codes[:, b, co, :].bitcast(FP8X4),
-                scales=x_scales[:, b, co, :],
-                in_=x_grouped[:, b, co, :, :].rearrange("p n t -> p (n t)"),
+                out=x_codes[:, b, groups, :].rearrange("p c n -> p (c n)").bitcast(FP8X4),
+                scales=x_scales[:, b, groups, :].rearrange("p c n -> p (c n)"),
+                in_=x_grouped[:, b, groups, :, :].rearrange("p c n t -> p (c n t)"),
             )
 
         prods = {}
@@ -241,50 +243,47 @@ def tile_scalarproductattentiont_pa_kernel(tc, nodes, W, out):
                 )
                 nc.sync.dma_start(out=out_rows[P * b : P * (b + 1), cols], in_=weights[:, cols])
 
+        for c in range(PASSES):
+            prepare_w(c, 0)
         pairs = BLOCKS // 2
-        for k in range(pairs + 1):
-            if k < pairs:
-                for b in (2 * k, 2 * k + 1):
-                    transpose_nodes(b)
-                    copy_nodes(nc.scalar.copy, b)
-                if k == 0:
-                    quantise_nodes(0, 1)
-                    quantise_nodes(1, 1)
-                    for c in range(PASSES):
-                        prepare_w(c, 0)
-                else:
-                    if k == 3:
-                        regroup(1, 1)
-                    quantise_nodes(2 * k, 2)
-                    if k == 3:
-                        quantise(1, 1)
-            if k > 0:
-                for b in (2 * k - 2, 2 * k - 1):
-                    if b == BLOCKS - 1:
-                        first_matmul(0, 1)
-                        copy_x(nc.scalar.copy, 0, 1)
+        for k in range(pairs):
+            for b in (2 * k, 2 * k + 1):
+                transpose_nodes(b)
+                copy_nodes(nc.scalar.copy, b)
+            if k == 0:
+                quantise_nodes(0, 1)
+                quantise_nodes(1, 1)
+            else:
+                quantise_nodes(2 * k, 2)
+            for b in range(2 * k - 2, 2 * k):
+                if 0 <= b < 6:
                     first_matmul(b, 0)
                     copy_x(nc.scalar.copy, b, 0)
-            if k == 1:
-                prepare_w(0, 1)
-            if k > 1:
-                quantise_x(2 * k - 4, 0)
-                quantise_x(2 * k - 3, 0)
-        quantise_x(BLOCKS - 2, 0)
-        quantise_x(0, 1)
-        quantise_x(BLOCKS - 1, 0)
+            if 1 <= k <= PASSES:
+                prepare_w(k - 1, 1)
 
+        def x_block(b):
+            if b >= 6:
+                first_matmul(b, 0)
+                copy_x(nc.vector.tensor_copy if False else nc.scalar.copy, b, 0)
+            first_matmul(b, 1)
+            copy_x(nc.vector.tensor_copy if False else nc.scalar.copy, b, 1)
+
+        for i in range(2):
+            x_block(i)
+            quantise_x(i, slice(0, GROUPS))
         for step in range(BLOCKS + 2):
-            i = step + 1
+            i = step + 2
             if i < BLOCKS:
-                first_matmul(i, 1)
-                copy_x(nc.vector.tensor_copy if i % 4 == 1 else nc.scalar.copy, i, 1)
+                x_block(i)
+            b = step - 2
+            if b >= 0:
+                add_sums(b)
             if step < BLOCKS:
                 second_matmul(step, 0)
                 find_shift(step, 0)
             if i < BLOCKS:
-                quantise_x(i, 1)
-            b = step - 2
+                quantise_x(i, slice(0, GROUPS))
             if b >= 0:
                 invert_sum(b)
             if step < BLOCKS:
@@ -296,4 +295,3 @@ def tile_scalarproductattentiont_pa_kernel(tc, nodes, W, out):
             if 0 <= b < BLOCKS:
                 for h in range(HALVES):
                     exponential(b, h)
-                add_sums(b)

@@ -33,7 +33,7 @@ def tile_scalarproductattentiont_pa_kernel(tc, nodes, W, out):
 
     with ExitStack() as ctx:
         keep = ctx.enter_context(tc.tile_pool(name="keep", bufs=1))
-        soft = ctx.enter_context(tc.tile_pool(name="soft", bufs=3))
+        soft = ctx.enter_context(tc.tile_pool(name="soft", bufs=6))
         x_banks = ctx.enter_context(tc.psum_pool(name="x_banks", bufs=3))
         banks = ctx.enter_context(tc.psum_pool(name="banks", bufs=5))
         ctx.enter_context(tc.manual_schedule())
@@ -99,17 +99,25 @@ def tile_scalarproductattentiont_pa_kernel(tc, nodes, W, out):
             )
 
         def prepare_w(c, co):
-            regroup(c, co)
+            regroup(c, co, range(PACK))
             quantise(c, co)
 
-        def regroup(c, co):
-            for t in range(PACK):
+        def regroup(c, co, slots):
+            for t in slots:
                 shared = co == 0 and t >= 2
                 regroup_w(nc.scalar.copy if shared else nc.vector.tensor_copy, c, co, t)
 
         def quantise(c, co):
             for pair in range(2):
                 quantise_w(c, co, pair)
+
+        zeros = keep.tile([P, BANK], BF16, name="zeros")
+        nc.vector.memset(zeros[:], 0.0)
+
+        def warm_clock(count):
+            idle = banks.tile([P, BANK], F32, tag="bank", name="idle")
+            for i in range(count):
+                nc.tensor.matmul(idle[:], lhsT=zeros[:, 0:P], rhs=zeros[:], start=True, stop=True)
 
         flipped = {}
 
@@ -190,12 +198,12 @@ def tile_scalarproductattentiont_pa_kernel(tc, nodes, W, out):
                 out=scaled[:],
                 in0=prods[b, h][:],
                 scalar1=-1.0 / 32.0,
-                scalar2=None if h == 0 else shift[b][:, 0:1],
+                scalar2=None if h == 0 else shift[b, 0][:, 0:1],
                 op0=ALU.mult,
                 op1=ALU.min,
                 accum_out=new[:],
             )
-            shift[b] = new
+            shift[b, h] = new
 
         expd = {}
         part_sum = {}
@@ -209,12 +217,23 @@ def tile_scalarproductattentiont_pa_kernel(tc, nodes, W, out):
                 out=expd[b][:, BANK * h : BANK * (h + 1)],
                 in_=prods[b, h][:],
                 func=ACT.Exp,
-                bias=shift[b][:, 0:1],
+                bias=shift[b, h][:, 0:1],
                 scale=1.0 / 32.0,
                 accum_out=part_sum[b][:, h : h + 1],
             )
 
+        rescale = {}
         row_sum = {}
+
+        def find_rescale(b):
+            rescale[b] = soft.tile([P, 1], F32, name="rescale")
+            nc.scalar.activation(
+                out=rescale[b][:],
+                in_=shift[b, 0][:],
+                func=ACT.Exp,
+                bias=shift[b, 1][:, 0:1],
+                scale=-1.0,
+            )
 
         def add_sums(b):
             row_sum[b] = soft.tile([P, 1], F32, name="row_sum")
@@ -222,6 +241,7 @@ def tile_scalarproductattentiont_pa_kernel(tc, nodes, W, out):
                 out=row_sum[b][:],
                 in_=part_sum[b][:, 0:1],
                 func=ACT.Identity,
+                scale=rescale[b][:, 0:1],
                 bias=part_sum[b][:, 1:2],
             )
 
@@ -230,26 +250,29 @@ def tile_scalarproductattentiont_pa_kernel(tc, nodes, W, out):
             nc.vector.reciprocal(out=inv_sum[b][:], in_=row_sum[b][:])
 
         def normalise(engine, b):
-            weights = soft.tile([P, NODES], F32, name="weights", bufs=5)
+            weights = soft.tile([P, NODES], F32, name="weights")
             for h in range(HALVES):
                 cols = slice(BANK * h, BANK * (h + 1))
                 engine.tensor_scalar(
                     out=weights[:, cols],
                     in0=expd[b][:, cols],
                     scalar1=inv_sum[b][:, 0:1],
-                    scalar2=0.0,
+                    scalar2=rescale[b][:, 0:1] if h == 0 else 1.0,
                     op0=ALU.mult,
-                    op1=ALU.add,
+                    op1=ALU.mult,
                 )
                 nc.sync.dma_start(out=out_rows[P * b : P * (b + 1), cols], in_=weights[:, cols])
 
         for c in range(PASSES):
             prepare_w(c, 0)
+        warm_clock(12)
         pairs = BLOCKS // 2
         for k in range(pairs):
             for b in (2 * k, 2 * k + 1):
                 transpose_nodes(b)
                 copy_nodes(nc.scalar.copy, b)
+            if 1 <= k <= PASSES:
+                regroup(k - 1, 1, (0, 1))
             if k == 0:
                 quantise_nodes(0, 1)
                 quantise_nodes(1, 1)
@@ -260,12 +283,17 @@ def tile_scalarproductattentiont_pa_kernel(tc, nodes, W, out):
                     first_matmul(b, 0)
                     copy_x(nc.scalar.copy, b, 0)
             if 1 <= k <= PASSES:
-                prepare_w(k - 1, 1)
+                regroup(k - 1, 1, (2, 3))
+                quantise(k - 1, 1)
+
+        for b in range(BLOCKS - 2, 6):
+            first_matmul(b, 0)
+            copy_x(nc.scalar.copy, b, 0)
 
         def x_block(b):
             if b >= 6:
                 first_matmul(b, 0)
-                copy_x(nc.vector.tensor_copy if False else nc.scalar.copy, b, 0)
+                copy_x(nc.vector.tensor_copy if True else nc.scalar.copy, b, 0)
             first_matmul(b, 1)
             copy_x(nc.vector.tensor_copy if False else nc.scalar.copy, b, 1)
 
@@ -282,10 +310,10 @@ def tile_scalarproductattentiont_pa_kernel(tc, nodes, W, out):
             if step < BLOCKS:
                 second_matmul(step, 0)
                 find_shift(step, 0)
-            if i < BLOCKS:
-                quantise_x(i, slice(0, GROUPS))
             if b >= 0:
                 invert_sum(b)
+            if i < BLOCKS:
+                quantise_x(i, slice(0, GROUPS))
             if step < BLOCKS:
                 second_matmul(step, 1)
                 find_shift(step, 1)
@@ -293,5 +321,6 @@ def tile_scalarproductattentiont_pa_kernel(tc, nodes, W, out):
                 normalise(nc.gpsimd if b < BLOCKS - 2 else nc.vector, b)
             b = step - 1
             if 0 <= b < BLOCKS:
-                for h in range(HALVES):
-                    exponential(b, h)
+                exponential(b, 0)
+                find_rescale(b)
+                exponential(b, 1)

@@ -265,7 +265,7 @@ def tile_scalarproductattentiont_pa_kernel(tc, nodes, W, out):
 
         for c in range(PASSES):
             prepare_w(c, 0)
-        warm_clock(12)
+        warm_clock(10)
         pairs = BLOCKS // 2
         for k in range(pairs):
             for b in (2 * k, 2 * k + 1):
@@ -279,16 +279,12 @@ def tile_scalarproductattentiont_pa_kernel(tc, nodes, W, out):
             else:
                 quantise_nodes(2 * k, 2)
             for b in range(2 * k - 2, 2 * k):
-                if 0 <= b < 6:
+                if 0 <= b < 4:
                     first_matmul(b, 0)
                     copy_x(nc.scalar.copy, b, 0)
             if 1 <= k <= PASSES:
                 regroup(k - 1, 1, (2, 3))
                 quantise(k - 1, 1)
-
-        for b in range(BLOCKS - 2, 6):
-            first_matmul(b, 0)
-            copy_x(nc.scalar.copy, b, 0)
 
         def x_block(b):
             if b >= 6:
@@ -298,7 +294,10 @@ def tile_scalarproductattentiont_pa_kernel(tc, nodes, W, out):
             copy_x(nc.vector.tensor_copy if False else nc.scalar.copy, b, 1)
 
         for i in range(2):
+            first_matmul(6 - 2 + i, 0)
+            copy_x(nc.scalar.copy, 6 - 2 + i, 0)
             x_block(i)
+        for i in range(2):
             quantise_x(i, slice(0, GROUPS))
         for step in range(BLOCKS + 2):
             i = step + 2

@@ -249,19 +249,21 @@ def tile_scalarproductattentiont_pa_kernel(tc, nodes, W, out):
             inv_sum[b] = soft.tile([P, 1], F32, name="inv_sum")
             nc.vector.reciprocal(out=inv_sum[b][:], in_=row_sum[b][:])
 
-        def normalise(engine, b):
-            weights = soft.tile([P, NODES], F32, name="weights")
-            for h in range(HALVES):
-                cols = slice(BANK * h, BANK * (h + 1))
-                engine.tensor_scalar(
-                    out=weights[:, cols],
-                    in0=expd[b][:, cols],
-                    scalar1=inv_sum[b][:, 0:1],
-                    scalar2=rescale[b][:, 0:1] if h == 0 else 1.0,
-                    op0=ALU.mult,
-                    op1=ALU.mult,
-                )
-                nc.sync.dma_start(out=out_rows[P * b : P * (b + 1), cols], in_=weights[:, cols])
+        weights = {}
+
+        def normalise(engine, b, h):
+            if h == 0:
+                weights[b] = soft.tile([P, NODES], F32, name="weights")
+            cols = slice(BANK * h, BANK * (h + 1))
+            engine.tensor_scalar(
+                out=weights[b][:, cols],
+                in0=expd[b][:, cols],
+                scalar1=inv_sum[b][:, 0:1],
+                scalar2=rescale[b][:, 0:1] if h == 0 else 1.0,
+                op0=ALU.mult,
+                op1=ALU.mult,
+            )
+            nc.sync.dma_start(out=out_rows[P * b : P * (b + 1), cols], in_=weights[b][:, cols])
 
         for c in range(PASSES):
             prepare_w(c, 0)
@@ -306,6 +308,7 @@ def tile_scalarproductattentiont_pa_kernel(tc, nodes, W, out):
             b = step - 2
             if b >= 0:
                 add_sums(b)
+                engine = nc.gpsimd if b < BLOCKS - 3 else nc.vector
             if step < BLOCKS:
                 second_matmul(step, 0)
                 find_shift(step, 0)
@@ -313,11 +316,13 @@ def tile_scalarproductattentiont_pa_kernel(tc, nodes, W, out):
                 invert_sum(b)
             if i < BLOCKS:
                 quantise_x(i, slice(0, GROUPS))
+            if b >= 0:
+                normalise(engine, b, 0)
             if step < BLOCKS:
                 second_matmul(step, 1)
                 find_shift(step, 1)
             if b >= 0:
-                normalise(nc.gpsimd if b < BLOCKS - 2 else nc.vector, b)
+                normalise(engine, b, 1)
             b = step - 1
             if 0 <= b < BLOCKS:
                 exponential(b, 0)

@@ -114,8 +114,9 @@ def tile_scalarproductattentiont_pa_kernel(tc, nodes, W, out):
         zeros = keep.tile([P, BANK], BF16, name="zeros")
         nc.vector.memset(zeros[:], 0.0)
 
+        idle = banks.tile([P, BANK], F32, tag="bank", name="idle")
+
         def warm_clock(count):
-            idle = banks.tile([P, BANK], F32, tag="bank", name="idle")
             for i in range(count):
                 nc.tensor.matmul(idle[:], lhsT=zeros[:, 0:P], rhs=zeros[:], start=True, stop=True)
 
@@ -267,12 +268,14 @@ def tile_scalarproductattentiont_pa_kernel(tc, nodes, W, out):
 
         for c in range(PASSES):
             prepare_w(c, 0)
-        warm_clock(10)
+        warm_clock(9)
         pairs = BLOCKS // 2
         for k in range(pairs):
             for b in (2 * k, 2 * k + 1):
                 transpose_nodes(b)
                 copy_nodes(nc.scalar.copy, b)
+                if b == 1:
+                    warm_clock(3)
             if 1 <= k <= PASSES:
                 regroup(k - 1, 1, (0, 1))
             if k == 0:

@@ -104,7 +104,7 @@ def tile_scalarproductattentiont_pa_kernel(tc, nodes, W, out):
 
         def regroup(c, co, slots):
             for t in slots:
-                shared = co == 0 and t >= 2
+                shared = co == 0 and t == 3
                 regroup_w(nc.scalar.copy if shared else nc.vector.tensor_copy, c, co, t)
 
         def quantise(c, co):

@@ -273,7 +273,7 @@ def tile_scalarproductattentiont_pa_kernel(tc, nodes, W, out):
         for k in range(pairs):
             for b in (2 * k, 2 * k + 1):
                 transpose_nodes(b)
-                copy_nodes(nc.scalar.copy, b)
+                copy_nodes(nc.vector.tensor_copy if b == BLOCKS - 1 else nc.scalar.copy, b)
                 if b == 1:
                     warm_clock(3)
             if 1 <= k <= PASSES:
@@ -312,10 +312,13 @@ def tile_scalarproductattentiont_pa_kernel(tc, nodes, W, out):
             if b >= 0:
                 add_sums(b)
                 engine = nc.gpsimd if b < BLOCKS - 3 else nc.vector
+            last = step == BLOCKS - 1
+            if last:
+                invert_sum(b)
             if step < BLOCKS:
                 second_matmul(step, 0)
                 find_shift(step, 0)
-            if b >= 0:
+            if b >= 0 and not last:
                 invert_sum(b)
             if i < BLOCKS:
                 quantise_x(i, slice(0, GROUPS))

from contextlib import ExitStack

import concourse.mybir as mybir
from concourse.masks import make_identity

BF16 = mybir.dt.bfloat16
F32 = mybir.dt.float32
U32 = mybir.dt.uint32
U8 = mybir.dt.uint8
FP8X4 = mybir.dt.float8_e4m3fn_x4
ACT = mybir.ActivationFunctionType
ALU = mybir.AluOpType
AXIS = mybir.AxisListType

P = 128
PACK = 4
K_PASS = P * PACK
NODES = 1024
FEATURES = 1024
PASSES = FEATURES // K_PASS
GROUPS = FEATURES // K_PASS
BLOCKS = NODES // P
BANK = 512
HALVES = NODES // BANK

FLOPS = 2 * 2 * NODES * FEATURES * FEATURES


def tile_scalarproductattentiont_pa_kernel(tc, nodes, W, out):
    nc = tc.nc
    node_rows = nodes.flatten_outer_dims()
    out_rows = out.flatten_outer_dims()

    with ExitStack() as ctx:
        keep = ctx.enter_context(tc.tile_pool(name="keep", bufs=1))
        soft = ctx.enter_context(tc.tile_pool(name="soft", bufs=6))
        x_banks = ctx.enter_context(tc.psum_pool(name="x_banks", bufs=3))
        banks = ctx.enter_context(tc.psum_pool(name="banks", bufs=5))
        ctx.enter_context(tc.manual_schedule())

        w_raw = keep.tile([P, PASSES, GROUPS, PACK, BANK], BF16, name="w_raw")
        w_grouped = keep.tile([P, PASSES, GROUPS, PACK, P * PACK], BF16, align_bytes=64, name="w_grouped")
        w_codes = keep.tile([P, PASSES, GROUPS, PACK, P], U32, align_bytes=64, name="w_codes")
        w_scales = keep.tile([P, PASSES, GROUPS, PACK, P], U8, align_bytes=64, name="w_scales")
        n_raw = keep.tile([P, BLOCKS, FEATURES], BF16, name="n_raw")
        n_words = n_raw[:].rearrange("p b f -> p (b f)").bitcast(F32)
        n_grouped = keep.tile([P, PASSES * NODES * PACK], BF16, align_bytes=64, name="n_grouped")
        n_grouped_words = n_grouped[:].bitcast(F32).rearrange("p (c n u) -> p c n u", c=PASSES, u=2)
        n_codes = keep.tile([P, PASSES, NODES], U32, align_bytes=64, name="n_codes")
        n_scales = keep.tile([P, PASSES, NODES], U8, align_bytes=64, name="n_scales")
        x_grouped = keep.tile([P, BLOCKS, GROUPS, P, PACK], BF16, align_bytes=64, name="x_grouped")
        x_codes = keep.tile([P, BLOCKS, GROUPS, P], U32, align_bytes=64, name="x_codes")
        x_scales = keep.tile([P, BLOCKS, GROUPS, P], U8, align_bytes=64, name="x_scales")

        def load_w(c, co):
            nc.sync.dma_start(
                out=w_raw[:, c, co, :, :],
                in_=W[K_PASS * c : K_PASS * (c + 1), BANK * co : BANK * (co + 1)].rearrange(
                    "(p t) g -> p t g", t=PACK
                ),
            )

        def load_nodes(b):
            nc.sync.dma_start(out=n_raw[:, b, :], in_=node_rows[P * b : P * (b + 1), :])

        load_w(0, 0)
        load_w(1, 0)
        load_nodes(0)
        load_nodes(1)
        load_nodes(2)
        load_nodes(3)
        load_w(0, 1)
        load_nodes(4)
        load_nodes(5)
        load_w(1, 1)
        load_nodes(6)
        load_nodes(7)

        ident = keep.tile([P, P], F32, name="ident")
        make_identity(nc, ident[:])

        warm_in = keep.tile([P, 1], F32, name="warm_in")
        warm_out = keep.tile([P, 1], F32, name="warm_out")
        nc.vector.memset(warm_in[:], 0.0)
        nc.scalar.activation(out=warm_out[:], in_=warm_in[:], func=ACT.Exp)

        def regroup_w(engine_copy, c, co, t):
            engine_copy(
                out=w_grouped[:, c, co, t, :].rearrange("p (r i j) -> p r j i", i=4, j=PACK),
                in_=w_raw[:, c, co, :, :].rearrange("p j (r i t) -> p t r j i", i=4, t=PACK)[:, t],
            )

        def quantise_w(c, co, pair):
            ts = slice(2 * pair, 2 * pair + 2)
            nc.vector.quantize_mx(
                out=w_codes[:, c, co, ts, :].rearrange("p t q -> p (t q)").bitcast(FP8X4),
                scales=w_scales[:, c, co, ts, :].rearrange("p t q -> p (t q)"),
                in_=w_grouped[:, c, co, ts, :].rearrange("p t q -> p (t q)"),
            )

        def prepare_w(c, co):
            regroup(c, co, range(PACK))
            quantise(c, co)

        def regroup(c, co, slots):
            for t in slots:
                shared = co == 0 and t == 3
                regroup_w(nc.scalar.copy if shared else nc.vector.tensor_copy, c, co, t)

        def quantise(c, co):
            for pair in range(2):
                quantise_w(c, co, pair)

        zeros = keep.tile([P, BANK], BF16, name="zeros")
        nc.vector.memset(zeros[:], 0.0)

        idle = banks.tile([P, BANK], F32, tag="bank", name="idle")

        def warm_clock(count):
            for i in range(count):
                nc.tensor.matmul(idle[:], lhsT=zeros[:, 0:P], rhs=zeros[:], start=True, stop=True)

        flipped = {}

        def transpose_nodes(b):
            flipped[b] = banks.tile([P, PASSES, 2, P], F32, tag="bank", name="flip")
            for c in range(PASSES):
                for u in range(2):
                    first_word = 512 * b + 256 * c
                    nc.tensor.transpose(
                        flipped[b][:, c, u, :],
                        n_words[:, first_word + u : first_word + 2 * P : 2],
                        ident[:],
                    )

        def copy_nodes(engine_copy, b):
            engine_copy(
                out=n_grouped_words[:, :, P * b : P * (b + 1), :],
                in_=flipped[b][:].rearrange("p c u n -> p c n u"),
            )

        def quantise_nodes(b, count):
            for c in range(PASSES):
                start = PACK * (NODES * c + P * b)
                nc.vector.quantize_mx(
                    out=n_codes[:, c, P * b : P * (b + count)].bitcast(FP8X4),
                    scales=n_scales[:, c, P * b : P * (b + count)],
                    in_=n_grouped[:, start : start + count * P * PACK],
                )

        xt = {}

        def first_matmul(b, co):
            xt[b, co] = x_banks.tile([P, PACK, P], F32, tag="xt", name="xt")
            for t in range(PACK):
                for c in range(PASSES):
                    nc.tensor.matmul_mx(
                        out=xt[b, co][:, t, :],
                        lhsT=w_codes[:, c, co, t, :].bitcast(FP8X4),
                        lhsT_scale=w_scales[:, c, co, t, :],
                        rhs=n_codes[:, c, P * b : P * (b + 1)].bitcast(FP8X4),
                        rhs_scale=n_scales[:, c, P * b : P * (b + 1)],
                        start=(c == 0),
                        stop=(c == PASSES - 1),
                    )

        def copy_x(engine_copy, b, co):
            engine_copy(
                out=x_grouped[:, b, co, :, :], in_=xt[b, co][:].rearrange("p t n -> p n t")
            )

        def quantise_x(b, groups):
            nc.vector.quantize_mx(
                out=x_codes[:, b, groups, :].rearrange("p c n -> p (c n)").bitcast(FP8X4),
                scales=x_scales[:, b, groups, :].rearrange("p c n -> p (c n)"),
                in_=x_grouped[:, b, groups, :, :].rearrange("p c n t -> p (c n t)"),
            )

        prods = {}
        shift = {}

        def second_matmul(b, h):
            prods[b, h] = banks.tile([P, BANK], F32, tag="bank", name="prod")
            for c in range(PASSES):
                nc.tensor.matmul_mx(
                    out=prods[b, h][:],
                    lhsT=x_codes[:, b, c, :].bitcast(FP8X4),
                    lhsT_scale=x_scales[:, b, c, :],
                    rhs=n_codes[:, c, BANK * h : BANK * (h + 1)].bitcast(FP8X4),
                    rhs_scale=n_scales[:, c, BANK * h : BANK * (h + 1)],
                    start=(c == 0),
                    stop=(c == PASSES - 1),
                )

        def find_shift(b, h):
            new = soft.tile([P, 1], F32, name="shift%d" % h)
            scaled = soft.tile([P, BANK], F32, name="scaled")
            nc.vector.tensor_scalar(
                out=scaled[:],
                in0=prods[b, h][:],
                scalar1=-1.0 / 32.0,
                scalar2=None if h == 0 else shift[b, 0][:, 0:1],
                op0=ALU.mult,
                op1=ALU.min,
                accum_out=new[:],
            )
            shift[b, h] = new

        expd = {}
        part_sum = {}
        inv_sum = {}

        def exponential(b, h):
            if h == 0:
                expd[b] = soft.tile([P, NODES], F32, name="expd")
                part_sum[b] = soft.tile([P, HALVES], F32, name="part_sum")
            nc.scalar.activation(
                out=expd[b][:, BANK * h : BANK * (h + 1)],
                in_=prods[b, h][:],
                func=ACT.Exp,
                bias=shift[b, h][:, 0:1],
                scale=1.0 / 32.0,
                accum_out=part_sum[b][:, h : h + 1],
            )

        rescale = {}
        row_sum = {}

        def find_rescale(b):
            rescale[b] = soft.tile([P, 1], F32, name="rescale")
            nc.scalar.activation(
                out=rescale[b][:],
                in_=shift[b, 0][:],
                func=ACT.Exp,
                bias=shift[b, 1][:, 0:1],
                scale=-1.0,
            )

        def add_sums(b):
            row_sum[b] = soft.tile([P, 1], F32, name="row_sum")
            nc.scalar.activation(
                out=row_sum[b][:],
                in_=part_sum[b][:, 0:1],
                func=ACT.Identity,
                scale=rescale[b][:, 0:1],
                bias=part_sum[b][:, 1:2],
            )

        def invert_sum(b):
            inv_sum[b] = soft.tile([P, 1], F32, name="inv_sum")
            nc.vector.reciprocal(out=inv_sum[b][:], in_=row_sum[b][:])

        weights = {}

        def normalise(engine, b, h):
            if h == 0:
                weights[b] = soft.tile([P, NODES], F32, name="weights")
            cols = slice(BANK * h, BANK * (h + 1))
            engine.tensor_scalar(
                out=weights[b][:, cols],
                in0=expd[b][:, cols],
                scalar1=inv_sum[b][:, 0:1],
                scalar2=rescale[b][:, 0:1] if h == 0 else 1.0,
                op0=ALU.mult,
                op1=ALU.mult,
            )
            nc.sync.dma_start(out=out_rows[P * b : P * (b + 1), cols], in_=weights[b][:, cols])

        for c in range(PASSES):
            prepare_w(c, 0)
        warm_clock(9)
        pairs = BLOCKS // 2
        for k in range(pairs):
            for b in (2 * k, 2 * k + 1):
                transpose_nodes(b)
                copy_nodes(nc.vector.tensor_copy if b == BLOCKS - 1 else nc.scalar.copy, b)
                if b == 1:
                    warm_clock(3)
            if 1 <= k <= PASSES:
                regroup(k - 1, 1, (0, 1))
            if k == 0:
                quantise_nodes(0, 1)
                quantise_nodes(1, 1)
            else:
                quantise_nodes(2 * k, 2)
            for b in range(2 * k - 2, 2 * k):
                if 0 <= b < 4:
                    first_matmul(b, 0)
                    copy_x(nc.scalar.copy, b, 0)
            if 1 <= k <= PASSES:
                regroup(k - 1, 1, (2, 3))
                quantise(k - 1, 1)

        def x_block(b):
            if b >= 6:
                first_matmul(b, 0)
                copy_x(nc.vector.tensor_copy if True else nc.scalar.copy, b, 0)
            first_matmul(b, 1)
            copy_x(nc.vector.tensor_copy if False else nc.scalar.copy, b, 1)

        for i in range(2):
            first_matmul(6 - 2 + i, 0)
            copy_x(nc.scalar.copy, 6 - 2 + i, 0)
            x_block(i)
        for i in range(2):
            quantise_x(i, slice(0, GROUPS))
        for step in range(BLOCKS + 2):
            i = step + 2
            if i < BLOCKS:
                x_block(i)
            b = step - 2
            if b >= 0:
                add_sums(b)
                engine = nc.gpsimd if b < BLOCKS - 3 else nc.vector
            last = step == BLOCKS - 1
            if last:
                invert_sum(b)
            if step < BLOCKS:
                second_matmul(step, 0)
                find_shift(step, 0)
            if b >= 0 and not last:
                invert_sum(b)
            if i < BLOCKS:
                quantise_x(i, slice(0, GROUPS))
            if b >= 0:
                normalise(engine, b, 0)
            if step < BLOCKS:
                second_matmul(step, 1)
                find_shift(step, 1)
            if b >= 0:
                normalise(engine, b, 1)
            b = step - 1
            if 0 <= b < BLOCKS:
                exponential(b, 0)
                find_rescale(b)
                exponential(b, 1)
